import numpy as np
import ml_dtypes


def mxq(x, axis, fmt="e4m3"):
    dtype, down = {"e4m3": (ml_dtypes.float8_e4m3fn, 7), "e5m2": (ml_dtypes.float8_e5m2, 14)}[fmt]
    v = np.moveaxis(np.asarray(x, np.float32).astype(ml_dtypes.bfloat16).astype(np.float64), axis, -1)
    blocks = v.reshape(v.shape[:-1] + (-1, 32))
    amax = np.abs(blocks).max(-1, keepdims=True)
    byte = np.maximum(np.where(amax > 0, np.frexp(amax)[1] - 1 + 127, 0) - down, 1)
    scale = np.exp2(byte - 127.0)
    codes = (blocks / scale).astype(np.float32).astype(dtype).astype(np.float64)
    return np.moveaxis((codes * scale).reshape(v.shape), -1, axis)


WIDE = False


def mx_kscale(k):
    if not WIDE:
        return np.ones(k)
    levels = np.array([10, -10, 5, -5, 0])
    if k % 512:
        return np.exp2(np.random.permutation(np.resize(levels, k // 32))).repeat(32)
    a = np.empty((k // 512, 16))
    for p in range(k // 512):
        a[p, :8] = np.random.permutation(np.resize(levels, 8))
        for g in range(8):
            far = levels[np.abs(levels - a[p, g]) >= 10]
            a[p, g + 8] = far[np.random.randint(len(far))]
    return np.exp2(a.ravel()).repeat(32)


BF16 = ml_dtypes.bfloat16


def bf(x):
    return np.asarray(x, np.float32).astype(BF16)


def f64(x):
    return np.asarray(x).astype(np.float64)


B, S, D, H, HD, M, G = 4, 768, 1536, 12, 128, 6144, 3
EPS = 1e-6
HH = H * HD


def silu(v):
    return v / (1.0 + np.exp(-v))


def rmsnorm(x, gain):
    var = np.mean(np.square(x), axis=-1, keepdims=True)
    return x * (1.0 / np.sqrt(var + EPS)) * gain


def setup_inputs():
    s, t = mx_kscale(HH), mx_kscale(D)
    return {"attn": bf(0.3 * np.random.standard_normal((B, S, HH)) * s),
            "x": bf(np.random.standard_normal((B, S, D))),
            "w_o": bf(np.random.standard_normal((HH, D)) * 2.0 / np.sqrt(HH) / s[:, None]),
            "rms2_scale": bf((1.0 + 0.1 * np.random.standard_normal(D)) * t),
            "w_gate": bf(np.random.standard_normal((D, M)) / np.sqrt(D) / t[:, None]),
            "w_up": bf(np.random.standard_normal((D, M)) / np.sqrt(D) / t[:, None])}


def reference(attn, x, w_o, rms2_scale, w_gate, w_up):
    x_mid = f64(x) + (mxq(f64(attn), 2, "e4m3") @ mxq(f64(w_o), 0, "e4m3"))
    hq = mxq(rmsnorm(x_mid, f64(rms2_scale)), 2, "e4m3")
    g = silu(hq @ mxq(f64(w_gate), 0, "e4m3")) * (hq @ mxq(f64(w_up), 0, "e4m3"))
    return x_mid, g

@@ -1,0 +1,321 @@
+from contextlib import ExitStack
+import math
+
+import concourse.mybir as mybir
+from concourse.masks import make_identity
+
+F32 = mybir.dt.float32
+BF16 = mybir.dt.bfloat16
+U32 = mybir.dt.uint32
+U8 = mybir.dt.uint8
+FP8X4 = mybir.dt.float8_e4m3fn_x4
+ACT = mybir.ActivationFunctionType
+ALU = mybir.AluOpType
+
+P = 128
+TOK = 3072
+D = 1536
+M = 6144
+EPS = 1e-6
+G = 3
+NW = 512
+NP = TOK // 256
+NCH = M // NW
+FLOPS = 2 * TOK * D * (D + 2 * M)
+
+LAG = 1
+K1 = 7
+WSLOTS = 9
+XV_HEAD = 288
+XV_1 = 224
+XV_2 = 256
+PACE = (2, 2, 2, 2, 2, 1, 1, 1, 1, 1, 1, 1, 1, 0, 0, 0, 0)
+
+
+def tile_transformerblocktpu_pb_l_kernel(tc, attn, x, w_o, rms2_scale, w_gate, w_up, out_0, out_1):
+    nc = tc.nc
+    attn_f = attn.flatten_outer_dims()
+    x_f = x.flatten_outer_dims()
+    o0_f = out_0.flatten_outer_dims()
+    o1_f = out_1.flatten_outer_dims()
+
+    with ExitStack() as ctx:
+        ctx.enter_context(tc.manual_schedule())
+        const = ctx.enter_context(tc.tile_pool(name="const", bufs=1))
+        keep = ctx.enter_context(tc.tile_pool(name="keep", bufs=1))
+        wpool = ctx.enter_context(tc.tile_pool(name="wpool", bufs=WSLOTS))
+        stage = ctx.enter_context(tc.tile_pool(name="stage", bufs=2))
+        psum = ctx.enter_context(tc.psum_pool(name="psum", bufs=8))
+
+        def bank():
+            return psum.tile([P, NW], F32, name="bank", tag="bank")
+
+        def six(name):
+            return stage.tile([P, 2 * D], BF16, name=name, tag="six", bufs=6, align_bytes=64)
+
+        warm = const.tile([P, 8], F32, name="warm")
+        nc.vector.memset(warm[:], 0.0)
+        nc.scalar.activation(out=warm[:, 0:1], in_=warm[:, 1:2], func=ACT.Silu)
+        ident = const.tile([P, P], F32, name="ident")
+        make_identity(nc, ident[:])
+        ones = const.tile([P, P], BF16, name="ones")
+        nc.vector.memset(ones[:], 1.0)
+        grow = six("grow")
+        nc.vector.memset(grow[:, 0:D], 0.0)
+        gsort = const.tile([P, G, 2, 256], BF16, name="gsort")
+        mhalf = const.tile([P, 2], F32, name="mhalf")
+        nc.vector.memset(mhalf[:], -0.5)
+
+        araw = {}
+        xraw = {}
+        xmid = {}
+
+        def load_attn(j):
+            araw[j] = six("araw").rearrange("p (i k) -> p i k", i=2)
+            nc.sync.dma_start(out=araw[j], in_=attn_f[256 * j:256 * (j + 1), :].rearrange("(i p) k -> p i k", p=P))
+
+        def load_x(j):
+            xraw[j] = six("xraw").rearrange("p (i k) -> p i k", i=2)
+            nc.sync.dma_start(out=xraw[j], in_=x_f[256 * j:256 * (j + 1), :].rearrange("(i p) k -> p i k", p=P))
+
+        wcodes = {}
+        wscale = {}
+        parts = []
+        for n in range(3):
+            for g in range(G):
+                parts.append((("o", n), g, w_o, NW * n))
+        for c in range(NCH):
+            for g in range(G):
+                parts.append((("g", c), g, w_gate, NW * c))
+                parts.append((("u", c), g, w_up, NW * c))
+        state = {"loaded": 0, "copied": 0, "quant": 0}
+        praw = {}
+        pgrp = {}
+
+        def part_load():
+            s = state["loaded"]
+            if s >= len(parts):
+                return
+            key, g, mat, c0 = parts[s]
+            praw[s] = stage.tile([P, 4, NW], BF16, name="praw", tag="praw", bufs=3)
+            nc.sync.dma_start(out=praw[s][:], in_=mat[NW * g:NW * (g + 1), c0:c0 + NW].rearrange("(p j) w -> p j w", j=4))
+            state["loaded"] = s + 1
+
+        def part_copy(xv):
+            s = state["copied"]
+            pgrp[s] = stage.tile([P, NW, 4], BF16, name="pgrp", tag="pgrp", bufs=2, align_bytes=64)
+            src = praw[s][:].rearrange("p j w -> p w j")
+            if xv > 0:
+                nc.vector.tensor_copy(out=pgrp[s][:, 0:xv, :], in_=src[:, 0:xv, :])
+            for lo in range(xv, NW, 256):
+                hi = min(NW, lo + 256)
+                nc.scalar.copy(out=pgrp[s][:, lo:hi, :], in_=src[:, lo:hi, :])
+            state["copied"] = s + 1
+            part_load()
+
+        def part_quant():
+            s = state["quant"]
+            key, g, mat, c0 = parts[s]
+            if key not in wcodes:
+                wcodes[key] = wpool.tile([P, G, NW], U32, name="wcodes", tag="wcodes", align_bytes=64)
+                wscale[key] = wpool.tile([P, G, NW], U8, name="wscale", tag="wscale", align_bytes=64)
+            nc.vector.quantize_mx(out=wcodes[key][:, g, :].bitcast(FP8X4), scales=wscale[key][:, g, :],
+                                  in_=pgrp[s][:].rearrange("p w j -> p (w j)"))
+            state["quant"] = s + 1
+
+        def prep(xv, limit):
+            if state["quant"] < state["copied"]:
+                part_quant()
+            if state["copied"] < min(limit, len(parts)):
+                part_copy(xv)
+
+        def prep_until(nparts, xv):
+            for r in range(2 * len(parts)):
+                if state["quant"] < nparts:
+                    prep(xv, nparts)
+
+        def chunk_parts(c):
+            return 9 + 6 * c
+
+        acodes = {}
+        ascale = {}
+        hcodes = {}
+        hscale = {}
+        rstd = {}
+        hsort = {}
+        tbank = {}
+        grouped = {}
+
+        def transposes(kind, j):
+            for g in range(G):
+                b = bank()
+                tbank[(kind, j, g)] = b
+                bv = b[:].rearrange("p (u r) -> p u r", u=2)
+                for i in range(2):
+                    for u in range(2):
+                        if kind == "a":
+                            src = araw[j][:, i, :].bitcast(F32)[:, 256 * g + u:256 * (g + 1):2]
+                        else:
+                            src = hsort[j][:, i, g, u, :].bitcast(F32)
+                        nc.tensor.transpose(bv[:, u, P * i:P * (i + 1)], src, ident[:])
+
+        def copies(kind, j):
+            for g in range(G):
+                t = stage.tile([P, 256, 4], BF16, name="grp", tag="grp", bufs=4, align_bytes=64)
+                grouped[(kind, j, g)] = t
+                nc.scalar.copy(out=t[:].bitcast(F32), in_=tbank[(kind, j, g)][:].rearrange("p (u r) -> p r u", u=2))
+
+        def quants(kind, j):
+            if kind == "a":
+                cod = stage.tile([P, G, 256], U32, name="acodes", tag="acodes", align_bytes=64)
+                sca = stage.tile([P, G, 256], U8, name="ascale", tag="ascale", align_bytes=64)
+                acodes[j] = cod
+                ascale[j] = sca
+            else:
+                cod = keep.tile([P, G, 256], U32, name="hcodes%d" % j, align_bytes=64)
+                sca = keep.tile([P, G, 256], U8, name="hscale%d" % j, align_bytes=64)
+                hcodes[j] = cod
+                hscale[j] = sca
+            for g in range(G):
+                nc.vector.quantize_mx(out=cod[:, g, :].bitcast(FP8X4), scales=sca[:, g, :],
+                                      in_=grouped[(kind, j, g)][:].rearrange("p r t -> p (r t)"))
+
+        def stage1_matmuls(j, after_bank):
+            xm = stage.tile([P, 2, D], F32, name="xmid", tag="xmid", bufs=2)
+            xmid[j] = xm
+            for i in range(2):
+                for n in range(3):
+                    b = bank()
+                    for g in range(G):
+                        nc.tensor.matmul_mx(out=b[:], lhsT=acodes[j][:, g, P * i:P * (i + 1)].bitcast(FP8X4),
+                                            lhsT_scale=ascale[j][:, g, P * i:P * (i + 1)],
+                                            rhs=wcodes[("o", n)][:, g, :].bitcast(FP8X4), rhs_scale=wscale[("o", n)][:, g, :],
+                                            start=(g == 0), stop=(g == G - 1))
+                    nc.vector.tensor_tensor(out=xm[:, i, NW * n:NW * (n + 1)], in0=b[:],
+                                            in1=xraw[j][:, i, NW * n:NW * (n + 1)], op=ALU.add)
+                    after_bank(3 * i + n)
+                if i == 0:
+                    squares(j, 0)
+            nc.sync.dma_start(out=o0_f[256 * j:256 * (j + 1), :].rearrange("(i p) d -> p i d", p=P), in_=xm[:])
+
+        def squares(j, i):
+            if i == 0:
+                rstd[j] = (stage.tile([P, 2], F32, name="ms", tag="ms"), stage.tile([P, 2], F32, name="rstd", tag="rstd", bufs=3))
+            junk = stage.tile([P, D], BF16, name="junk", tag="junk", bufs=1)
+            nc.scalar.activation(out=junk[:], in_=xmid[j][:, i, :], func=ACT.Square, scale=1.0 / math.sqrt(D),
+                                 accum_out=rstd[j][0][:, i:i + 1])
+            if i == 1:
+                nc.gpsimd.tensor_scalar(out=rstd[j][0][:], in0=rstd[j][0][:], scalar1=1.0, scalar2=EPS, op0=ALU.mult, op1=ALU.add)
+                nc.gpsimd.tensor_tensor(out=rstd[j][1][:], in0=rstd[j][0][:], in1=mhalf[:], op=ALU.pow)
+
+        def normed(j, i):
+            if i == 0:
+                hsort[j] = six("hsort").rearrange("p (i g u w) -> p i g u w", i=2, g=G, u=2)
+            for g in range(G):
+                xv = xmid[j][:, i, NW * g:NW * (g + 1)].rearrange("p (m u e) -> p u m e", u=2, e=2)
+                for u in range(2):
+                    nc.vector.scalar_tensor_tensor(out=hsort[j][:, i, g, u, :].rearrange("p (m e) -> p m e", e=2),
+                                                   in0=xv[:, u], scalar=rstd[j][1][:, i:i + 1],
+                                                   in1=gsort[:, g, u, :].rearrange("p (m e) -> p m e", e=2),
+                                                   op0=ALU.mult, op1=ALU.mult)
+
+        def unit(c, t):
+            j, i = t // 2, t % 2
+            bg = bank()
+            bu = bank()
+            for key, b in ((("g", c), bg), (("u", c), bu)):
+                for g in range(G):
+                    nc.tensor.matmul_mx(out=b[:], lhsT=hcodes[j][:, g, P * i:P * (i + 1)].bitcast(FP8X4),
+                                        lhsT_scale=hscale[j][:, g, P * i:P * (i + 1)],
+                                        rhs=wcodes[key][:, g, :].bitcast(FP8X4), rhs_scale=wscale[key][:, g, :],
+                                        start=(g == 0), stop=(g == G - 1))
+            sg = stage.tile([P, NW], F32, name="sg", tag="sg", bufs=3)
+            nc.scalar.activation(out=sg[:], in_=bg[:], func=ACT.Silu)
+            go = stage.tile([P, NW], F32, name="go", tag="go", bufs=3)
+            nc.vector.tensor_tensor(out=go[:], in0=bu[:], in1=sg[:], op=ALU.mult)
+            nc.sync.dma_start(out=o1_f[P * t:P * (t + 1), NW * c:NW * (c + 1)], in_=go[:])
+
+        load_attn(0)
+        for s in range(3):
+            part_load()
+        load_x(0)
+        load_attn(1)
+        nc.sync.dma_start(out=grow[0:1, 0:D], in_=rms2_scale.rearrange("(o d) -> o d", o=1))
+
+        transposes("a", 0)
+        copies("a", 0)
+        prep_until(3, XV_HEAD)
+        quants("a", 0)
+        prep_until(9, XV_HEAD)
+
+        lim1 = chunk_parts(3)
+        for k in range(NP + LAG + 3):
+            jn, jh, ju = k - LAG, k - LAG - 1, k - LAG - 2
+            todo = {"n": PACE[k]}
+
+            def step():
+                if todo["n"] > 0:
+                    todo["n"] -= 1
+                    prep(XV_1, lim1)
+
+            if k + 1 < NP:
+                load_x(k + 1)
+            if k + 2 < NP:
+                load_attn(k + 2)
+            if k + 1 < NP:
+                transposes("a", k + 1)
+                copies("a", k + 1)
+            if 0 <= jh < NP:
+                transposes("h", jh)
+            if k + 1 < NP:
+                quants("a", k + 1)
+            if 0 <= jh < NP:
+                copies("h", jh)
+                quants("h", jh)
+            if k < NP:
+                stage1_matmuls(k, lambda q: step() if (q in (1, 4) and ju < 0) else None)
+            if k == 0:
+                for g in range(G):
+                    b = bank()
+                    nc.tensor.matmul(b[:], lhsT=ones[:], rhs=grow[:, NW * g:NW * (g + 1)], start=True, stop=True)
+                    nc.vector.tensor_copy(out=gsort[:, g].rearrange("p u (m e) -> p u m e", e=2),
+                                          in_=b[:].rearrange("p (m u e) -> p u m e", u=2, e=2))
+            units = []
+            if 0 <= ju < NP:
+                for t in (2 * ju, 2 * ju + 1):
+                    units.append((0, t))
+                    if k >= K1:
+                        units.append((1, t))
+            extras = []
+            if k < NP:
+                extras.append(lambda: squares(k, 1))
+            if 0 <= jn < NP:
+                extras.append(lambda: normed(jn, 0))
+                extras.append(lambda: normed(jn, 1))
+            if not units:
+                for e in extras:
+                    e()
+            if units:
+                prep_until(chunk_parts(2 if k >= K1 else 1), XV_1)
+            for q, (c, t) in enumerate(units):
+                unit(c, t)
+                if q == 0:
+                    for e in extras[0:2]:
+                        e()
+                elif q == 1:
+                    for e in extras[2:]:
+                        e()
+                    step()
+                else:
+                    step()
+        prep_until(chunk_parts(2), XV_1)
+        for t in range(2 * (K1 - LAG - 2)):
+            unit(1, t)
+            if t % 2 == 0:
+                prep(XV_2, chunk_parts(4))
+        for c in range(2, NCH):
+            prep_until(chunk_parts(c + 1), XV_2)
+            for t in range(2 * NP):
+                unit(c, t)
+                if t % 3 == 2:
+                    prep(XV_2, chunk_parts(c + 3))

@@ -26,6 +26,8 @@ FLOPS = 2 * TOK * D * (D + 2 * M)
 LAG = 1
 K1 = 7
 WSLOTS = 9
+GO_BUFS = 8
+PRAW_BUFS = 4
 XV_HEAD = 288
 XV_1 = 224
 XV_2 = 256
@@ -50,8 +52,8 @@ def tile_transformerblocktpu_pb_l_kernel(tc, attn, x, w_o, rms2_scale, w_gate, w
         def bank():
             return psum.tile([P, NW], F32, name="bank", tag="bank")
 
-        def six(name):
-            return stage.tile([P, 2 * D], BF16, name=name, tag="six", bufs=6, align_bytes=64)
+        def six(name, bufs):
+            return stage.tile([P, 2 * D], BF16, name=name, tag=name, bufs=bufs, align_bytes=64)
 
         warm = const.tile([P, 8], F32, name="warm")
         nc.vector.memset(warm[:], 0.0)
@@ -60,9 +62,9 @@ def tile_transformerblocktpu_pb_l_kernel(tc, attn, x, w_o, rms2_scale, w_gate, w
         make_identity(nc, ident[:])
         ones = const.tile([P, P], BF16, name="ones")
         nc.vector.memset(ones[:], 1.0)
-        grow = six("grow")
+        grow = six("hsort", 2)
         nc.vector.memset(grow[:, 0:D], 0.0)
-        gsort = const.tile([P, G, 2, 256], BF16, name="gsort")
+        gsort = const.tile([P, 2, G, 256], BF16, name="gsort")
         mhalf = const.tile([P, 2], F32, name="mhalf")
         nc.vector.memset(mhalf[:], -0.5)
 
@@ -71,19 +73,16 @@ def tile_transformerblocktpu_pb_l_kernel(tc, attn, x, w_o, rms2_scale, w_gate, w
         xmid = {}
 
         def load_attn(j):
-            araw[j] = six("araw").rearrange("p (i k) -> p i k", i=2)
+            araw[j] = six("araw", 3).rearrange("p (i k) -> p i k", i=2)
             nc.sync.dma_start(out=araw[j], in_=attn_f[256 * j:256 * (j + 1), :].rearrange("(i p) k -> p i k", p=P))
 
         def load_x(j):
-            xraw[j] = six("xraw").rearrange("p (i k) -> p i k", i=2)
+            xraw[j] = six("xraw", 2).rearrange("p (i k) -> p i k", i=2)
             nc.sync.dma_start(out=xraw[j], in_=x_f[256 * j:256 * (j + 1), :].rearrange("(i p) k -> p i k", p=P))
 
         wcodes = {}
         wscale = {}
         parts = []
-        for n in range(3):
-            for g in range(G):
-                parts.append((("o", n), g, w_o, NW * n))
         for c in range(NCH):
             for g in range(G):
                 parts.append((("g", c), g, w_gate, NW * c))
@@ -97,12 +96,13 @@ def tile_transformerblocktpu_pb_l_kernel(tc, attn, x, w_o, rms2_scale, w_gate, w
             if s >= len(parts):
                 return
             key, g, mat, c0 = parts[s]
-            praw[s] = stage.tile([P, 4, NW], BF16, name="praw", tag="praw", bufs=3)
+            praw[s] = stage.tile([P, 4, NW], BF16, name="praw", tag="praw", bufs=PRAW_BUFS)
             nc.sync.dma_start(out=praw[s][:], in_=mat[NW * g:NW * (g + 1), c0:c0 + NW].rearrange("(p j) w -> p j w", j=4))
             state["loaded"] = s + 1
 
         def part_copy(xv):
             s = state["copied"]
+            part_load()
             pgrp[s] = stage.tile([P, NW, 4], BF16, name="pgrp", tag="pgrp", bufs=2, align_bytes=64)
             src = praw[s][:].rearrange("p j w -> p w j")
             if xv > 0:
@@ -111,15 +111,14 @@ def tile_transformerblocktpu_pb_l_kernel(tc, attn, x, w_o, rms2_scale, w_gate, w
                 hi = min(NW, lo + 256)
                 nc.scalar.copy(out=pgrp[s][:, lo:hi, :], in_=src[:, lo:hi, :])
             state["copied"] = s + 1
-            part_load()
 
         def part_quant():
             s = state["quant"]
             key, g, mat, c0 = parts[s]
             if key not in wcodes:
                 wcodes[key] = wpool.tile([P, G, NW], U32, name="wcodes", tag="wcodes", align_bytes=64)
-                wscale[key] = wpool.tile([P, G, NW], U8, name="wscale", tag="wscale", align_bytes=64)
-            nc.vector.quantize_mx(out=wcodes[key][:, g, :].bitcast(FP8X4), scales=wscale[key][:, g, :],
+                wscale[key] = wpool.tile([P, NW], U8, name="wscale", tag="wscale", align_bytes=64)
+            nc.vector.quantize_mx(out=wcodes[key][:, g, :].bitcast(FP8X4), scales=wscale[key][4 * g:P, :],
                                   in_=pgrp[s][:].rearrange("p w j -> p (w j)"))
             state["quant"] = s + 1
 
@@ -135,7 +134,29 @@ def tile_transformerblocktpu_pb_l_kernel(tc, attn, x, w_o, rms2_scale, w_gate, w
                     prep(xv, nparts)
 
         def chunk_parts(c):
-            return 9 + 6 * c
+            return 6 * c
+
+        slab = {}
+        ogrp = {}
+
+        def load_slab(g):
+            slab[g] = keep.tile([P, 4, D], BF16, name="slab%d" % g, align_bytes=64, offset=12288 * g)
+            nc.sync.dma_start(out=slab[g][:], in_=w_o[NW * g:NW * (g + 1), :].rearrange("(p j) w -> p j w", j=4))
+
+        def wo_copy(g, n):
+            t = stage.tile([P, NW, 4], BF16, name="pgrp", tag="pgrp", bufs=2, align_bytes=64)
+            ogrp[(g, n)] = t
+            src = slab[g][:, :, NW * n:NW * (n + 1)].rearrange("p j w -> p w j")
+            nc.vector.tensor_copy(out=t[:, 0:XV_HEAD, :], in_=src[:, 0:XV_HEAD, :])
+            nc.scalar.copy(out=t[:, XV_HEAD:NW, :], in_=src[:, XV_HEAD:NW, :])
+
+        def wo_quant(g, n):
+            key = ("o", n)
+            if key not in wcodes:
+                wcodes[key] = wpool.tile([P, G, NW], U32, name="wcodes", tag="wcodes", align_bytes=64)
+                wscale[key] = wpool.tile([P, NW], U8, name="wscale", tag="wscale", align_bytes=64)
+            nc.vector.quantize_mx(out=wcodes[key][:, g, :].bitcast(FP8X4), scales=wscale[key][4 * g:P, :],
+                                  in_=ogrp[(g, n)][:].rearrange("p w j -> p (w j)"))
 
         acodes = {}
         ascale = {}
@@ -156,7 +177,7 @@ def tile_transformerblocktpu_pb_l_kernel(tc, attn, x, w_o, rms2_scale, w_gate, w
                         if kind == "a":
                             src = araw[j][:, i, :].bitcast(F32)[:, 256 * g + u:256 * (g + 1):2]
                         else:
-                            src = hsort[j][:, i, g, u, :].bitcast(F32)
+                            src = hsort[j][:, i, u, g, :].bitcast(F32)
                         nc.tensor.transpose(bv[:, u, P * i:P * (i + 1)], src, ident[:])
 
         def copies(kind, j):
@@ -168,16 +189,16 @@ def tile_transformerblocktpu_pb_l_kernel(tc, attn, x, w_o, rms2_scale, w_gate, w
         def quants(kind, j):
             if kind == "a":
                 cod = stage.tile([P, G, 256], U32, name="acodes", tag="acodes", align_bytes=64)
-                sca = stage.tile([P, G, 256], U8, name="ascale", tag="ascale", align_bytes=64)
+                sca = stage.tile([P, 256], U8, name="ascale", tag="ascale", align_bytes=64)
                 acodes[j] = cod
                 ascale[j] = sca
             else:
-                cod = keep.tile([P, G, 256], U32, name="hcodes%d" % j, align_bytes=64)
-                sca = keep.tile([P, G, 256], U8, name="hscale%d" % j, align_bytes=64)
+                cod = keep.tile([P, G, 256], U32, name="hcodes%d" % j, align_bytes=64, offset=3328 * j)
+                sca = keep.tile([P, 256], U8, name="hscale%d" % j, align_bytes=64, offset=3328 * j + 3072)
                 hcodes[j] = cod
                 hscale[j] = sca
             for g in range(G):
-                nc.vector.quantize_mx(out=cod[:, g, :].bitcast(FP8X4), scales=sca[:, g, :],
+                nc.vector.quantize_mx(out=cod[:, g, :].bitcast(FP8X4), scales=sca[4 * g:P, :],
                                       in_=grouped[(kind, j, g)][:].rearrange("p r t -> p (r t)"))
 
         def stage1_matmuls(j, after_bank):
@@ -188,15 +209,15 @@ def tile_transformerblocktpu_pb_l_kernel(tc, attn, x, w_o, rms2_scale, w_gate, w
                     b = bank()
                     for g in range(G):
                         nc.tensor.matmul_mx(out=b[:], lhsT=acodes[j][:, g, P * i:P * (i + 1)].bitcast(FP8X4),
-                                            lhsT_scale=ascale[j][:, g, P * i:P * (i + 1)],
-                                            rhs=wcodes[("o", n)][:, g, :].bitcast(FP8X4), rhs_scale=wscale[("o", n)][:, g, :],
+                                            lhsT_scale=ascale[j][4 * g:P, P * i:P * (i + 1)],
+                                            rhs=wcodes[("o", n)][:, g, :].bitcast(FP8X4), rhs_scale=wscale[("o", n)][4 * g:P, :],
                                             start=(g == 0), stop=(g == G - 1))
                     nc.vector.tensor_tensor(out=xm[:, i, NW * n:NW * (n + 1)], in0=b[:],
                                             in1=xraw[j][:, i, NW * n:NW * (n + 1)], op=ALU.add)
                     after_bank(3 * i + n)
+                nc.sync.dma_start(out=o0_f[256 * j + P * i:256 * j + P * (i + 1), :], in_=xm[:, i, :])
                 if i == 0:
                     squares(j, 0)
-            nc.sync.dma_start(out=o0_f[256 * j:256 * (j + 1), :].rearrange("(i p) d -> p i d", p=P), in_=xm[:])
 
         def squares(j, i):
             if i == 0:
@@ -210,14 +231,13 @@ def tile_transformerblocktpu_pb_l_kernel(tc, attn, x, w_o, rms2_scale, w_gate, w
 
         def normed(j, i):
             if i == 0:
-                hsort[j] = six("hsort").rearrange("p (i g u w) -> p i g u w", i=2, g=G, u=2)
-            for g in range(G):
-                xv = xmid[j][:, i, NW * g:NW * (g + 1)].rearrange("p (m u e) -> p u m e", u=2, e=2)
-                for u in range(2):
-                    nc.vector.scalar_tensor_tensor(out=hsort[j][:, i, g, u, :].rearrange("p (m e) -> p m e", e=2),
-                                                   in0=xv[:, u], scalar=rstd[j][1][:, i:i + 1],
-                                                   in1=gsort[:, g, u, :].rearrange("p (m e) -> p m e", e=2),
-                                                   op0=ALU.mult, op1=ALU.mult)
+                hsort[j] = six("hsort", 2).rearrange("p (i u g w) -> p i u g w", i=2, g=G, u=2)
+            xv = xmid[j][:, i, :].rearrange("p (m u e) -> p u m e", u=2, e=2)
+            for u in range(2):
+                nc.vector.scalar_tensor_tensor(out=hsort[j][:, i, u].rearrange("p g (m e) -> p (g m) e", e=2),
+                                               in0=xv[:, u], scalar=rstd[j][1][:, i:i + 1],
+                                               in1=gsort[:, u].rearrange("p g (m e) -> p (g m) e", e=2),
+                                               op0=ALU.mult, op1=ALU.mult)
 
         def unit(c, t):
             j, i = t // 2, t % 2
@@ -226,27 +246,34 @@ def tile_transformerblocktpu_pb_l_kernel(tc, attn, x, w_o, rms2_scale, w_gate, w
             for key, b in ((("g", c), bg), (("u", c), bu)):
                 for g in range(G):
                     nc.tensor.matmul_mx(out=b[:], lhsT=hcodes[j][:, g, P * i:P * (i + 1)].bitcast(FP8X4),
-                                        lhsT_scale=hscale[j][:, g, P * i:P * (i + 1)],
-                                        rhs=wcodes[key][:, g, :].bitcast(FP8X4), rhs_scale=wscale[key][:, g, :],
+                                        lhsT_scale=hscale[j][4 * g:P, P * i:P * (i + 1)],
+                                        rhs=wcodes[key][:, g, :].bitcast(FP8X4), rhs_scale=wscale[key][4 * g:P, :],
                                         start=(g == 0), stop=(g == G - 1))
             sg = stage.tile([P, NW], F32, name="sg", tag="sg", bufs=3)
             nc.scalar.activation(out=sg[:], in_=bg[:], func=ACT.Silu)
-            go = stage.tile([P, NW], F32, name="go", tag="go", bufs=3)
+            go = stage.tile([P, NW], F32, name="go", tag="go", bufs=GO_BUFS)
             nc.vector.tensor_tensor(out=go[:], in0=bu[:], in1=sg[:], op=ALU.mult)
             nc.sync.dma_start(out=o1_f[P * t:P * (t + 1), NW * c:NW * (c + 1)], in_=go[:])
 
         load_attn(0)
-        for s in range(3):
-            part_load()
-        load_x(0)
+        for g in range(G):
+            load_slab(g)
         load_attn(1)
+        load_x(0)
+        load_attn(2)
         nc.sync.dma_start(out=grow[0:1, 0:D], in_=rms2_scale.rearrange("(o d) -> o d", o=1))
+        for s in range(PRAW_BUFS - 1):
+            part_load()
 
         transposes("a", 0)
         copies("a", 0)
-        prep_until(3, XV_HEAD)
         quants("a", 0)
-        prep_until(9, XV_HEAD)
+        order = [(g, n) for g in range(G) for n in range(3)]
+        for s in range(len(order) + 1):
+            if s < len(order):
+                wo_copy(order[s][0], order[s][1])
+            if s > 0:
+                wo_quant(order[s - 1][0], order[s - 1][1])
 
         lim1 = chunk_parts(3)
         for k in range(NP + LAG + 3):
@@ -258,10 +285,10 @@ def tile_transformerblocktpu_pb_l_kernel(tc, attn, x, w_o, rms2_scale, w_gate, w
                     todo["n"] -= 1
                     prep(XV_1, lim1)
 
+            if k + 3 < NP:
+                load_attn(k + 3)
             if k + 1 < NP:
                 load_x(k + 1)
-            if k + 2 < NP:
-                load_attn(k + 2)
             if k + 1 < NP:
                 transposes("a", k + 1)
                 copies("a", k + 1)
@@ -278,7 +305,7 @@ def tile_transformerblocktpu_pb_l_kernel(tc, attn, x, w_o, rms2_scale, w_gate, w
                 for g in range(G):
                     b = bank()
                     nc.tensor.matmul(b[:], lhsT=ones[:], rhs=grow[:, NW * g:NW * (g + 1)], start=True, stop=True)
-                    nc.vector.tensor_copy(out=gsort[:, g].rearrange("p u (m e) -> p u m e", e=2),
+                    nc.vector.tensor_copy(out=gsort[:, :, g, :].rearrange("p u (m e) -> p u m e", e=2),
                                           in_=b[:].rearrange("p (m u e) -> p u m e", u=2, e=2))
             units = []
             if 0 <= ju < NP:

@@ -24,10 +24,13 @@ NCH = M // NW
 FLOPS = 2 * TOK * D * (D + 2 * M)
 
 LAG = 1
-K1 = 7
+K1 = 8
 WSLOTS = 9
-GO_BUFS = 8
-PRAW_BUFS = 4
+COPY_FIRST = True
+PAD_RC = 0
+PAD_RS = 64
+PAD_LC = 128
+PAD_LS = 192
 XV_HEAD = 288
 XV_1 = 224
 XV_2 = 256
@@ -52,8 +55,16 @@ def tile_transformerblocktpu_pb_l_kernel(tc, attn, x, w_o, rms2_scale, w_gate, w
         def bank():
             return psum.tile([P, NW], F32, name="bank", tag="bank")
 
-        def six(name, bufs):
-            return stage.tile([P, 2 * D], BF16, name=name, tag=name, bufs=bufs, align_bytes=64)
+        def six(name):
+            return stage.tile([P, 2 * D], BF16, name=name, tag="six", bufs=6, align_bytes=64)
+
+        def code_tile(pool, width, pad, name, tag):
+            t = pool.tile([P, pad // 4 + G * width], U32, name=name, tag=tag, align_bytes=256)
+            return t[:, pad // 4:pad // 4 + G * width].rearrange("p (g w) -> p g w", g=G)
+
+        def plane_tile(pool, width, pad, name, tag):
+            t = pool.tile([P, pad + width], U8, name=name, tag=tag, align_bytes=256)
+            return t[:, pad:pad + width]
 
         warm = const.tile([P, 8], F32, name="warm")
         nc.vector.memset(warm[:], 0.0)
@@ -62,9 +73,9 @@ def tile_transformerblocktpu_pb_l_kernel(tc, attn, x, w_o, rms2_scale, w_gate, w
         make_identity(nc, ident[:])
         ones = const.tile([P, P], BF16, name="ones")
         nc.vector.memset(ones[:], 1.0)
-        grow = six("hsort", 2)
+        grow = six("grow")
         nc.vector.memset(grow[:, 0:D], 0.0)
-        gsort = const.tile([P, 2, G, 256], BF16, name="gsort")
+        gsort = const.tile([P, G, 2, 256], BF16, name="gsort")
         mhalf = const.tile([P, 2], F32, name="mhalf")
         nc.vector.memset(mhalf[:], -0.5)
 
@@ -73,16 +84,19 @@ def tile_transformerblocktpu_pb_l_kernel(tc, attn, x, w_o, rms2_scale, w_gate, w
         xmid = {}
 
         def load_attn(j):
-            araw[j] = six("araw", 3).rearrange("p (i k) -> p i k", i=2)
+            araw[j] = six("araw").rearrange("p (i k) -> p i k", i=2)
             nc.sync.dma_start(out=araw[j], in_=attn_f[256 * j:256 * (j + 1), :].rearrange("(i p) k -> p i k", p=P))
 
         def load_x(j):
-            xraw[j] = six("xraw", 2).rearrange("p (i k) -> p i k", i=2)
+            xraw[j] = six("xraw").rearrange("p (i k) -> p i k", i=2)
             nc.sync.dma_start(out=xraw[j], in_=x_f[256 * j:256 * (j + 1), :].rearrange("(i p) k -> p i k", p=P))
 
         wcodes = {}
         wscale = {}
         parts = []
+        for n in range(3):
+            for g in range(G):
+                parts.append((("o", n), g, w_o, NW * n))
         for c in range(NCH):
             for g in range(G):
                 parts.append((("g", c), g, w_gate, NW * c))
@@ -96,13 +110,12 @@ def tile_transformerblocktpu_pb_l_kernel(tc, attn, x, w_o, rms2_scale, w_gate, w
             if s >= len(parts):
                 return
             key, g, mat, c0 = parts[s]
-            praw[s] = stage.tile([P, 4, NW], BF16, name="praw", tag="praw", bufs=PRAW_BUFS)
+            praw[s] = stage.tile([P, 4, NW], BF16, name="praw", tag="praw", bufs=3)
             nc.sync.dma_start(out=praw[s][:], in_=mat[NW * g:NW * (g + 1), c0:c0 + NW].rearrange("(p j) w -> p j w", j=4))
             state["loaded"] = s + 1
 
         def part_copy(xv):
             s = state["copied"]
-            part_load()
             pgrp[s] = stage.tile([P, NW, 4], BF16, name="pgrp", tag="pgrp", bufs=2, align_bytes=64)
             src = praw[s][:].rearrange("p j w -> p w j")
             if xv > 0:
@@ -111,22 +124,26 @@ def tile_transformerblocktpu_pb_l_kernel(tc, attn, x, w_o, rms2_scale, w_gate, w
                 hi = min(NW, lo + 256)
                 nc.scalar.copy(out=pgrp[s][:, lo:hi, :], in_=src[:, lo:hi, :])
             state["copied"] = s + 1
+            part_load()
 
         def part_quant():
             s = state["quant"]
             key, g, mat, c0 = parts[s]
             if key not in wcodes:
-                wcodes[key] = wpool.tile([P, G, NW], U32, name="wcodes", tag="wcodes", align_bytes=64)
-                wscale[key] = wpool.tile([P, NW], U8, name="wscale", tag="wscale", align_bytes=64)
+                wcodes[key] = code_tile(wpool, NW, PAD_RC, "wcodes", "wcodes")
+                wscale[key] = plane_tile(wpool, NW, PAD_RS, "wscale", "wscale")
             nc.vector.quantize_mx(out=wcodes[key][:, g, :].bitcast(FP8X4), scales=wscale[key][4 * g:P, :],
                                   in_=pgrp[s][:].rearrange("p w j -> p (w j)"))
             state["quant"] = s + 1
 
         def prep(xv, limit):
-            if state["quant"] < state["copied"]:
+            behind = state["quant"] < state["copied"]
+            if behind and not COPY_FIRST:
                 part_quant()
             if state["copied"] < min(limit, len(parts)):
                 part_copy(xv)
+            if behind and COPY_FIRST:
+                part_quant()
 
         def prep_until(nparts, xv):
             for r in range(2 * len(parts)):
@@ -134,29 +151,7 @@ def tile_transformerblocktpu_pb_l_kernel(tc, attn, x, w_o, rms2_scale, w_gate, w
                     prep(xv, nparts)
 
         def chunk_parts(c):
-            return 6 * c
-
-        slab = {}
-        ogrp = {}
-
-        def load_slab(g):
-            slab[g] = keep.tile([P, 4, D], BF16, name="slab%d" % g, align_bytes=64, offset=12288 * g)
-            nc.sync.dma_start(out=slab[g][:], in_=w_o[NW * g:NW * (g + 1), :].rearrange("(p j) w -> p j w", j=4))
-
-        def wo_copy(g, n):
-            t = stage.tile([P, NW, 4], BF16, name="pgrp", tag="pgrp", bufs=2, align_bytes=64)
-            ogrp[(g, n)] = t
-            src = slab[g][:, :, NW * n:NW * (n + 1)].rearrange("p j w -> p w j")
-            nc.vector.tensor_copy(out=t[:, 0:XV_HEAD, :], in_=src[:, 0:XV_HEAD, :])
-            nc.scalar.copy(out=t[:, XV_HEAD:NW, :], in_=src[:, XV_HEAD:NW, :])
-
-        def wo_quant(g, n):
-            key = ("o", n)
-            if key not in wcodes:
-                wcodes[key] = wpool.tile([P, G, NW], U32, name="wcodes", tag="wcodes", align_bytes=64)
-                wscale[key] = wpool.tile([P, NW], U8, name="wscale", tag="wscale", align_bytes=64)
-            nc.vector.quantize_mx(out=wcodes[key][:, g, :].bitcast(FP8X4), scales=wscale[key][4 * g:P, :],
-                                  in_=ogrp[(g, n)][:].rearrange("p w j -> p (w j)"))
+            return 9 + 6 * c
 
         acodes = {}
         ascale = {}
@@ -177,7 +172,7 @@ def tile_transformerblocktpu_pb_l_kernel(tc, attn, x, w_o, rms2_scale, w_gate, w
                         if kind == "a":
                             src = araw[j][:, i, :].bitcast(F32)[:, 256 * g + u:256 * (g + 1):2]
                         else:
-                            src = hsort[j][:, i, u, g, :].bitcast(F32)
+                            src = hsort[j][:, i, g, u, :].bitcast(F32)
                         nc.tensor.transpose(bv[:, u, P * i:P * (i + 1)], src, ident[:])
 
         def copies(kind, j):
@@ -188,13 +183,13 @@ def tile_transformerblocktpu_pb_l_kernel(tc, attn, x, w_o, rms2_scale, w_gate, w
 
         def quants(kind, j):
             if kind == "a":
-                cod = stage.tile([P, G, 256], U32, name="acodes", tag="acodes", align_bytes=64)
-                sca = stage.tile([P, 256], U8, name="ascale", tag="ascale", align_bytes=64)
+                cod = code_tile(stage, 256, PAD_LC, "acodes", "acodes")
+                sca = plane_tile(stage, 256, PAD_LS, "ascale", "ascale")
                 acodes[j] = cod
                 ascale[j] = sca
             else:
-                cod = keep.tile([P, G, 256], U32, name="hcodes%d" % j, align_bytes=64, offset=3328 * j)
-                sca = keep.tile([P, 256], U8, name="hscale%d" % j, align_bytes=64, offset=3328 * j + 3072)
+                cod = code_tile(keep, 256, PAD_LC, "hcodes%d" % j, "hcodes%d" % j)
+                sca = plane_tile(keep, 256, PAD_LS, "hscale%d" % j, "hscale%d" % j)
                 hcodes[j] = cod
                 hscale[j] = sca
             for g in range(G):
@@ -215,9 +210,9 @@ def tile_transformerblocktpu_pb_l_kernel(tc, attn, x, w_o, rms2_scale, w_gate, w
                     nc.vector.tensor_tensor(out=xm[:, i, NW * n:NW * (n + 1)], in0=b[:],
                                             in1=xraw[j][:, i, NW * n:NW * (n + 1)], op=ALU.add)
                     after_bank(3 * i + n)
-                nc.sync.dma_start(out=o0_f[256 * j + P * i:256 * j + P * (i + 1), :], in_=xm[:, i, :])
                 if i == 0:
                     squares(j, 0)
+            nc.sync.dma_start(out=o0_f[256 * j:256 * (j + 1), :].rearrange("(i p) d -> p i d", p=P), in_=xm[:])
 
         def squares(j, i):
             if i == 0:
@@ -231,13 +226,14 @@ def tile_transformerblocktpu_pb_l_kernel(tc, attn, x, w_o, rms2_scale, w_gate, w
 
         def normed(j, i):
             if i == 0:
-                hsort[j] = six("hsort", 2).rearrange("p (i u g w) -> p i u g w", i=2, g=G, u=2)
-            xv = xmid[j][:, i, :].rearrange("p (m u e) -> p u m e", u=2, e=2)
-            for u in range(2):
-                nc.vector.scalar_tensor_tensor(out=hsort[j][:, i, u].rearrange("p g (m e) -> p (g m) e", e=2),
-                                               in0=xv[:, u], scalar=rstd[j][1][:, i:i + 1],
-                                               in1=gsort[:, u].rearrange("p g (m e) -> p (g m) e", e=2),
-                                               op0=ALU.mult, op1=ALU.mult)
+                hsort[j] = six("hsort").rearrange("p (i g u w) -> p i g u w", i=2, g=G, u=2)
+            for g in range(G):
+                xv = xmid[j][:, i, NW * g:NW * (g + 1)].rearrange("p (m u e) -> p u m e", u=2, e=2)
+                for u in range(2):
+                    nc.vector.scalar_tensor_tensor(out=hsort[j][:, i, g, u, :].rearrange("p (m e) -> p m e", e=2),
+                                                   in0=xv[:, u], scalar=rstd[j][1][:, i:i + 1],
+                                                   in1=gsort[:, g, u, :].rearrange("p (m e) -> p m e", e=2),
+                                                   op0=ALU.mult, op1=ALU.mult)
 
         def unit(c, t):
             j, i = t // 2, t % 2
@@ -251,29 +247,22 @@ def tile_transformerblocktpu_pb_l_kernel(tc, attn, x, w_o, rms2_scale, w_gate, w
                                         start=(g == 0), stop=(g == G - 1))
             sg = stage.tile([P, NW], F32, name="sg", tag="sg", bufs=3)
             nc.scalar.activation(out=sg[:], in_=bg[:], func=ACT.Silu)
-            go = stage.tile([P, NW], F32, name="go", tag="go", bufs=GO_BUFS)
+            go = stage.tile([P, NW], F32, name="go", tag="go", bufs=3)
             nc.vector.tensor_tensor(out=go[:], in0=bu[:], in1=sg[:], op=ALU.mult)
             nc.sync.dma_start(out=o1_f[P * t:P * (t + 1), NW * c:NW * (c + 1)], in_=go[:])
 
         load_attn(0)
-        for g in range(G):
-            load_slab(g)
-        load_attn(1)
-        load_x(0)
-        load_attn(2)
-        nc.sync.dma_start(out=grow[0:1, 0:D], in_=rms2_scale.rearrange("(o d) -> o d", o=1))
-        for s in range(PRAW_BUFS - 1):
+        for s in range(3):
             part_load()
+        load_x(0)
+        load_attn(1)
+        nc.sync.dma_start(out=grow[0:1, 0:D], in_=rms2_scale.rearrange("(o d) -> o d", o=1))
 
         transposes("a", 0)
         copies("a", 0)
+        prep_until(3, XV_HEAD)
         quants("a", 0)
-        order = [(g, n) for g in range(G) for n in range(3)]
-        for s in range(len(order) + 1):
-            if s < len(order):
-                wo_copy(order[s][0], order[s][1])
-            if s > 0:
-                wo_quant(order[s - 1][0], order[s - 1][1])
+        prep_until(9, XV_HEAD)
 
         lim1 = chunk_parts(3)
         for k in range(NP + LAG + 3):
@@ -285,10 +274,10 @@ def tile_transformerblocktpu_pb_l_kernel(tc, attn, x, w_o, rms2_scale, w_gate, w
                     todo["n"] -= 1
                     prep(XV_1, lim1)
 
-            if k + 3 < NP:
-                load_attn(k + 3)
             if k + 1 < NP:
                 load_x(k + 1)
+            if k + 2 < NP:
+                load_attn(k + 2)
             if k + 1 < NP:
                 transposes("a", k + 1)
                 copies("a", k + 1)
@@ -305,7 +294,7 @@ def tile_transformerblocktpu_pb_l_kernel(tc, attn, x, w_o, rms2_scale, w_gate, w
                 for g in range(G):
                     b = bank()
                     nc.tensor.matmul(b[:], lhsT=ones[:], rhs=grow[:, NW * g:NW * (g + 1)], start=True, stop=True)
-                    nc.vector.tensor_copy(out=gsort[:, :, g, :].rearrange("p u (m e) -> p u m e", e=2),
+                    nc.vector.tensor_copy(out=gsort[:, g].rearrange("p u (m e) -> p u m e", e=2),
                                           in_=b[:].rearrange("p (m u e) -> p u m e", u=2, e=2))
             units = []
             if 0 <= ju < NP:

@@ -27,10 +27,6 @@ LAG = 1
 K1 = 8
 WSLOTS = 9
 COPY_FIRST = True
-PAD_RC = 0
-PAD_RS = 64
-PAD_LC = 128
-PAD_LS = 192
 XV_HEAD = 288
 XV_1 = 224
 XV_2 = 256
@@ -57,14 +53,6 @@ def tile_transformerblocktpu_pb_l_kernel(tc, attn, x, w_o, rms2_scale, w_gate, w
 
         def six(name):
             return stage.tile([P, 2 * D], BF16, name=name, tag="six", bufs=6, align_bytes=64)
-
-        def code_tile(pool, width, pad, name, tag):
-            t = pool.tile([P, pad // 4 + G * width], U32, name=name, tag=tag, align_bytes=256)
-            return t[:, pad // 4:pad // 4 + G * width].rearrange("p (g w) -> p g w", g=G)
-
-        def plane_tile(pool, width, pad, name, tag):
-            t = pool.tile([P, pad + width], U8, name=name, tag=tag, align_bytes=256)
-            return t[:, pad:pad + width]
 
         warm = const.tile([P, 8], F32, name="warm")
         nc.vector.memset(warm[:], 0.0)
@@ -117,12 +105,13 @@ def tile_transformerblocktpu_pb_l_kernel(tc, attn, x, w_o, rms2_scale, w_gate, w
         def part_copy(xv):
             s = state["copied"]
             pgrp[s] = stage.tile([P, NW, 4], BF16, name="pgrp", tag="pgrp", bufs=2, align_bytes=64)
-            src = praw[s][:].rearrange("p j w -> p w j")
             if xv > 0:
-                nc.vector.tensor_copy(out=pgrp[s][:, 0:xv, :], in_=src[:, 0:xv, :])
+                nc.vector.tensor_copy(out=pgrp[s][:, 0:xv, :].rearrange("p (c i) j -> p c j i", i=4),
+                                      in_=praw[s][:, :, 0:xv].rearrange("p j (c i) -> p c j i", i=4))
             for lo in range(xv, NW, 256):
                 hi = min(NW, lo + 256)
-                nc.scalar.copy(out=pgrp[s][:, lo:hi, :], in_=src[:, lo:hi, :])
+                nc.scalar.copy(out=pgrp[s][:, lo:hi, :].rearrange("p (c i) j -> p c j i", i=4),
+                               in_=praw[s][:, :, lo:hi].rearrange("p j (c i) -> p c j i", i=4))
             state["copied"] = s + 1
             part_load()
 
@@ -130,9 +119,9 @@ def tile_transformerblocktpu_pb_l_kernel(tc, attn, x, w_o, rms2_scale, w_gate, w
             s = state["quant"]
             key, g, mat, c0 = parts[s]
             if key not in wcodes:
-                wcodes[key] = code_tile(wpool, NW, PAD_RC, "wcodes", "wcodes")
-                wscale[key] = plane_tile(wpool, NW, PAD_RS, "wscale", "wscale")
-            nc.vector.quantize_mx(out=wcodes[key][:, g, :].bitcast(FP8X4), scales=wscale[key][4 * g:P, :],
+                wcodes[key] = wpool.tile([P, G, NW], U32, name="wcodes", tag="wcodes", align_bytes=64)
+                wscale[key] = wpool.tile([P, G, NW], U8, name="wscale", tag="wscale", align_bytes=64)
+            nc.vector.quantize_mx(out=wcodes[key][:, g, :].bitcast(FP8X4), scales=wscale[key][:, g, :],
                                   in_=pgrp[s][:].rearrange("p w j -> p (w j)"))
             state["quant"] = s + 1
 
@@ -183,17 +172,17 @@ def tile_transformerblocktpu_pb_l_kernel(tc, attn, x, w_o, rms2_scale, w_gate, w
 
         def quants(kind, j):
             if kind == "a":
-                cod = code_tile(stage, 256, PAD_LC, "acodes", "acodes")
-                sca = plane_tile(stage, 256, PAD_LS, "ascale", "ascale")
+                cod = stage.tile([P, G, 256], U32, name="acodes", tag="acodes", align_bytes=64)
+                sca = stage.tile([P, G, 256], U8, name="ascale", tag="ascale", align_bytes=64)
                 acodes[j] = cod
                 ascale[j] = sca
             else:
-                cod = code_tile(keep, 256, PAD_LC, "hcodes%d" % j, "hcodes%d" % j)
-                sca = plane_tile(keep, 256, PAD_LS, "hscale%d" % j, "hscale%d" % j)
+                cod = keep.tile([P, G, 256], U32, name="hcodes%d" % j, align_bytes=64)
+                sca = keep.tile([P, G, 256], U8, name="hscale%d" % j, align_bytes=64)
                 hcodes[j] = cod
                 hscale[j] = sca
             for g in range(G):
-                nc.vector.quantize_mx(out=cod[:, g, :].bitcast(FP8X4), scales=sca[4 * g:P, :],
+                nc.vector.quantize_mx(out=cod[:, g, :].bitcast(FP8X4), scales=sca[:, g, :],
                                       in_=grouped[(kind, j, g)][:].rearrange("p r t -> p (r t)"))
 
         def stage1_matmuls(j, after_bank):
@@ -204,8 +193,8 @@ def tile_transformerblocktpu_pb_l_kernel(tc, attn, x, w_o, rms2_scale, w_gate, w
                     b = bank()
                     for g in range(G):
                         nc.tensor.matmul_mx(out=b[:], lhsT=acodes[j][:, g, P * i:P * (i + 1)].bitcast(FP8X4),
-                                            lhsT_scale=ascale[j][4 * g:P, P * i:P * (i + 1)],
-                                            rhs=wcodes[("o", n)][:, g, :].bitcast(FP8X4), rhs_scale=wscale[("o", n)][4 * g:P, :],
+                                            lhsT_scale=ascale[j][:, g, P * i:P * (i + 1)],
+                                            rhs=wcodes[("o", n)][:, g, :].bitcast(FP8X4), rhs_scale=wscale[("o", n)][:, g, :],
                                             start=(g == 0), stop=(g == G - 1))
                     nc.vector.tensor_tensor(out=xm[:, i, NW * n:NW * (n + 1)], in0=b[:],
                                             in1=xraw[j][:, i, NW * n:NW * (n + 1)], op=ALU.add)
@@ -242,8 +231,8 @@ def tile_transformerblocktpu_pb_l_kernel(tc, attn, x, w_o, rms2_scale, w_gate, w
             for key, b in ((("g", c), bg), (("u", c), bu)):
                 for g in range(G):
                     nc.tensor.matmul_mx(out=b[:], lhsT=hcodes[j][:, g, P * i:P * (i + 1)].bitcast(FP8X4),
-                                        lhsT_scale=hscale[j][4 * g:P, P * i:P * (i + 1)],
-                                        rhs=wcodes[key][:, g, :].bitcast(FP8X4), rhs_scale=wscale[key][4 * g:P, :],
+                                        lhsT_scale=hscale[j][:, g, P * i:P * (i + 1)],
+                                        rhs=wcodes[key][:, g, :].bitcast(FP8X4), rhs_scale=wscale[key][:, g, :],
                                         start=(g == 0), stop=(g == G - 1))
             sg = stage.tile([P, NW], F32, name="sg", tag="sg", bufs=3)
             nc.scalar.activation(out=sg[:], in_=bg[:], func=ACT.Silu)

@@ -119,8 +119,8 @@ def tile_transformerblocktpu_pb_l_kernel(tc, attn, x, w_o, rms2_scale, w_gate, w
             s = state["quant"]
             key, g, mat, c0 = parts[s]
             if key not in wcodes:
-                wcodes[key] = wpool.tile([P, G, NW], U32, name="wcodes", tag="wcodes", align_bytes=64)
-                wscale[key] = wpool.tile([P, G, NW], U8, name="wscale", tag="wscale", align_bytes=64)
+                wcodes[key] = wpool.tile([P, G, NW], U32, name="wcodes", tag="wcodes", align_bytes=256)
+                wscale[key] = wpool.tile([P, G, NW], U8, name="wscale", tag="wscale", align_bytes=256)
             nc.vector.quantize_mx(out=wcodes[key][:, g, :].bitcast(FP8X4), scales=wscale[key][:, g, :],
                                   in_=pgrp[s][:].rearrange("p w j -> p (w j)"))
             state["quant"] = s + 1
@@ -172,13 +172,13 @@ def tile_transformerblocktpu_pb_l_kernel(tc, attn, x, w_o, rms2_scale, w_gate, w
 
         def quants(kind, j):
             if kind == "a":
-                cod = stage.tile([P, G, 256], U32, name="acodes", tag="acodes", align_bytes=64)
-                sca = stage.tile([P, G, 256], U8, name="ascale", tag="ascale", align_bytes=64)
+                cod = stage.tile([P, G, 256], U32, name="acodes", tag="acodes", align_bytes=256)
+                sca = stage.tile([P, G, 256], U8, name="ascale", tag="ascale", align_bytes=256)
                 acodes[j] = cod
                 ascale[j] = sca
             else:
-                cod = keep.tile([P, G, 256], U32, name="hcodes%d" % j, align_bytes=64)
-                sca = keep.tile([P, G, 256], U8, name="hscale%d" % j, align_bytes=64)
+                cod = keep.tile([P, G, 256], U32, name="hcodes%d" % j, align_bytes=256)
+                sca = keep.tile([P, G, 256], U8, name="hscale%d" % j, align_bytes=256)
                 hcodes[j] = cod
                 hscale[j] = sca
             for g in range(G):

from contextlib import ExitStack
import math

import concourse.mybir as mybir
from concourse.masks import make_identity

F32 = mybir.dt.float32
BF16 = mybir.dt.bfloat16
U32 = mybir.dt.uint32
U8 = mybir.dt.uint8
FP8X4 = mybir.dt.float8_e4m3fn_x4
ACT = mybir.ActivationFunctionType
ALU = mybir.AluOpType

P = 128
TOK = 3072
D = 1536
M = 6144
EPS = 1e-6
G = 3
NW = 512
NP = TOK // 256
NCH = M // NW
FLOPS = 2 * TOK * D * (D + 2 * M)

LAG = 1
K1 = 8
WSLOTS = 9
COPY_FIRST = True
XV_HEAD = 288
XV_1 = 224
XV_2 = 256
PACE = (2, 2, 2, 2, 2, 1, 1, 1, 1, 1, 1, 1, 1, 0, 0, 0, 0)


def tile_transformerblocktpu_pb_l_kernel(tc, attn, x, w_o, rms2_scale, w_gate, w_up, out_0, out_1):
    nc = tc.nc
    attn_f = attn.flatten_outer_dims()
    x_f = x.flatten_outer_dims()
    o0_f = out_0.flatten_outer_dims()
    o1_f = out_1.flatten_outer_dims()

    with ExitStack() as ctx:
        ctx.enter_context(tc.manual_schedule())
        const = ctx.enter_context(tc.tile_pool(name="const", bufs=1))
        keep = ctx.enter_context(tc.tile_pool(name="keep", bufs=1))
        wpool = ctx.enter_context(tc.tile_pool(name="wpool", bufs=WSLOTS))
        stage = ctx.enter_context(tc.tile_pool(name="stage", bufs=2))
        psum = ctx.enter_context(tc.psum_pool(name="psum", bufs=8))

        def bank():
            return psum.tile([P, NW], F32, name="bank", tag="bank")

        def six(name):
            return stage.tile([P, 2 * D], BF16, name=name, tag="six", bufs=6, align_bytes=64)

        warm = const.tile([P, 8], F32, name="warm")
        nc.vector.memset(warm[:], 0.0)
        nc.scalar.activation(out=warm[:, 0:1], in_=warm[:, 1:2], func=ACT.Silu)
        ident = const.tile([P, P], F32, name="ident")
        make_identity(nc, ident[:])
        ones = const.tile([P, P], BF16, name="ones")
        nc.vector.memset(ones[:], 1.0)
        grow = six("grow")
        nc.vector.memset(grow[:, 0:D], 0.0)
        gsort = const.tile([P, G, 2, 256], BF16, name="gsort")
        mhalf = const.tile([P, 2], F32, name="mhalf")
        nc.vector.memset(mhalf[:], -0.5)

        araw = {}
        xraw = {}
        xmid = {}

        def load_attn(j):
            araw[j] = six("araw").rearrange("p (i k) -> p i k", i=2)
            nc.sync.dma_start(out=araw[j], in_=attn_f[256 * j:256 * (j + 1), :].rearrange("(i p) k -> p i k", p=P))

        def load_x(j):
            xraw[j] = six("xraw").rearrange("p (i k) -> p i k", i=2)
            nc.sync.dma_start(out=xraw[j], in_=x_f[256 * j:256 * (j + 1), :].rearrange("(i p) k -> p i k", p=P))

        wcodes = {}
        wscale = {}
        parts = []
        for n in range(3):
            for g in range(G):
                parts.append((("o", n), g, w_o, NW * n))
        for c in range(NCH):
            for g in range(G):
                parts.append((("g", c), g, w_gate, NW * c))
                parts.append((("u", c), g, w_up, NW * c))
        state = {"loaded": 0, "copied": 0, "quant": 0}
        praw = {}
        pgrp = {}

        def part_load():
            s = state["loaded"]
            if s >= len(parts):
                return
            key, g, mat, c0 = parts[s]
            praw[s] = stage.tile([P, 4, NW], BF16, name="praw", tag="praw", bufs=3)
            nc.sync.dma_start(out=praw[s][:], in_=mat[NW * g:NW * (g + 1), c0:c0 + NW].rearrange("(p j) w -> p j w", j=4))
            state["loaded"] = s + 1

        def part_copy(xv):
            s = state["copied"]
            pgrp[s] = stage.tile([P, NW, 4], BF16, name="pgrp", tag="pgrp", bufs=2, align_bytes=64)
            if xv > 0:
                nc.vector.tensor_copy(out=pgrp[s][:, 0:xv, :].rearrange("p (c i) j -> p c j i", i=4),
                                      in_=praw[s][:, :, 0:xv].rearrange("p j (c i) -> p c j i", i=4))
            for lo in range(xv, NW, 256):
                hi = min(NW, lo + 256)
                nc.scalar.copy(out=pgrp[s][:, lo:hi, :].rearrange("p (c i) j -> p c j i", i=4),
                               in_=praw[s][:, :, lo:hi].rearrange("p j (c i) -> p c j i", i=4))
            state["copied"] = s + 1
            part_load()

        def part_quant():
            s = state["quant"]
            key, g, mat, c0 = parts[s]
            if key not in wcodes:
                wcodes[key] = wpool.tile([P, G, NW], U32, name="wcodes", tag="wcodes", align_bytes=256)
                wscale[key] = wpool.tile([P, G, NW], U8, name="wscale", tag="wscale", align_bytes=256)
            nc.vector.quantize_mx(out=wcodes[key][:, g, :].bitcast(FP8X4), scales=wscale[key][:, g, :],
                                  in_=pgrp[s][:].rearrange("p w j -> p (w j)"))
            state["quant"] = s + 1

        def prep(xv, limit):
            behind = state["quant"] < state["copied"]
            if behind and not COPY_FIRST:
                part_quant()
            if state["copied"] < min(limit, len(parts)):
                part_copy(xv)
            if behind and COPY_FIRST:
                part_quant()

        def prep_until(nparts, xv):
            for r in range(2 * len(parts)):
                if state["quant"] < nparts:
                    prep(xv, nparts)

        def chunk_parts(c):
            return 9 + 6 * c

        acodes = {}
        ascale = {}
        hcodes = {}
        hscale = {}
        rstd = {}
        hsort = {}
        tbank = {}
        grouped = {}

        def transposes(kind, j):
            for g in range(G):
                b = bank()
                tbank[(kind, j, g)] = b
                bv = b[:].rearrange("p (u r) -> p u r", u=2)
                for i in range(2):
                    for u in range(2):
                        if kind == "a":
                            src = araw[j][:, i, :].bitcast(F32)[:, 256 * g + u:256 * (g + 1):2]
                        else:
                            src = hsort[j][:, i, g, u, :].bitcast(F32)
                        nc.tensor.transpose(bv[:, u, P * i:P * (i + 1)], src, ident[:])

        def copies(kind, j):
            for g in range(G):
                t = stage.tile([P, 256, 4], BF16, name="grp", tag="grp", bufs=4, align_bytes=64)
                grouped[(kind, j, g)] = t
                nc.scalar.copy(out=t[:].bitcast(F32), in_=tbank[(kind, j, g)][:].rearrange("p (u r) -> p r u", u=2))

        def quants(kind, j):
            if kind == "a":
                cod = stage.tile([P, G, 256], U32, name="acodes", tag="acodes", align_bytes=256)
                sca = stage.tile([P, G, 256], U8, name="ascale", tag="ascale", align_bytes=256)
                acodes[j] = cod
                ascale[j] = sca
            else:
                cod = keep.tile([P, G, 256], U32, name="hcodes%d" % j, align_bytes=256)
                sca = keep.tile([P, G, 256], U8, name="hscale%d" % j, align_bytes=256)
                hcodes[j] = cod
                hscale[j] = sca
            for g in range(G):
                nc.vector.quantize_mx(out=cod[:, g, :].bitcast(FP8X4), scales=sca[:, g, :],
                                      in_=grouped[(kind, j, g)][:].rearrange("p r t -> p (r t)"))

        def stage1_matmuls(j, after_bank):
            xm = stage.tile([P, 2, D], F32, name="xmid", tag="xmid", bufs=2)
            xmid[j] = xm
            for i in range(2):
                for n in range(3):
                    b = bank()
                    for g in range(G):
                        nc.tensor.matmul_mx(out=b[:], lhsT=acodes[j][:, g, P * i:P * (i + 1)].bitcast(FP8X4),
                                            lhsT_scale=ascale[j][:, g, P * i:P * (i + 1)],
                                            rhs=wcodes[("o", n)][:, g, :].bitcast(FP8X4), rhs_scale=wscale[("o", n)][:, g, :],
                                            start=(g == 0), stop=(g == G - 1))
                    nc.vector.tensor_tensor(out=xm[:, i, NW * n:NW * (n + 1)], in0=b[:],
                                            in1=xraw[j][:, i, NW * n:NW * (n + 1)], op=ALU.add)
                    after_bank(3 * i + n)
                if i == 0:
                    squares(j, 0)
            nc.sync.dma_start(out=o0_f[256 * j:256 * (j + 1), :].rearrange("(i p) d -> p i d", p=P), in_=xm[:])

        def squares(j, i):
            if i == 0:
                rstd[j] = (stage.tile([P, 2], F32, name="ms", tag="ms"), stage.tile([P, 2], F32, name="rstd", tag="rstd", bufs=3))
            junk = stage.tile([P, D], BF16, name="junk", tag="junk", bufs=1)
            nc.scalar.activation(out=junk[:], in_=xmid[j][:, i, :], func=ACT.Square, scale=1.0 / math.sqrt(D),
                                 accum_out=rstd[j][0][:, i:i + 1])
            if i == 1:
                nc.gpsimd.tensor_scalar(out=rstd[j][0][:], in0=rstd[j][0][:], scalar1=1.0, scalar2=EPS, op0=ALU.mult, op1=ALU.add)
                nc.gpsimd.tensor_tensor(out=rstd[j][1][:], in0=rstd[j][0][:], in1=mhalf[:], op=ALU.pow)

        def normed(j, i):
            if i == 0:
                hsort[j] = six("hsort").rearrange("p (i g u w) -> p i g u w", i=2, g=G, u=2)
            for g in range(G):
                xv = xmid[j][:, i, NW * g:NW * (g + 1)].rearrange("p (m u e) -> p u m e", u=2, e=2)
                for u in range(2):
                    nc.vector.scalar_tensor_tensor(out=hsort[j][:, i, g, u, :].rearrange("p (m e) -> p m e", e=2),
                                                   in0=xv[:, u], scalar=rstd[j][1][:, i:i + 1],
                                                   in1=gsort[:, g, u, :].rearrange("p (m e) -> p m e", e=2),
                                                   op0=ALU.mult, op1=ALU.mult)

        def unit(c, t):
            j, i = t // 2, t % 2
            bg = bank()
            bu = bank()
            for key, b in ((("g", c), bg), (("u", c), bu)):
                for g in range(G):
                    nc.tensor.matmul_mx(out=b[:], lhsT=hcodes[j][:, g, P * i:P * (i + 1)].bitcast(FP8X4),
                                        lhsT_scale=hscale[j][:, g, P * i:P * (i + 1)],
                                        rhs=wcodes[key][:, g, :].bitcast(FP8X4), rhs_scale=wscale[key][:, g, :],
                                        start=(g == 0), stop=(g == G - 1))
            sg = stage.tile([P, NW], F32, name="sg", tag="sg", bufs=3)
            nc.scalar.activation(out=sg[:], in_=bg[:], func=ACT.Silu)
            go = stage.tile([P, NW], F32, name="go", tag="go", bufs=3)
            nc.vector.tensor_tensor(out=go[:], in0=bu[:], in1=sg[:], op=ALU.mult)
            nc.sync.dma_start(out=o1_f[P * t:P * (t + 1), NW * c:NW * (c + 1)], in_=go[:])

        load_attn(0)
        for s in range(3):
            part_load()
        load_x(0)
        load_attn(1)
        nc.sync.dma_start(out=grow[0:1, 0:D], in_=rms2_scale.rearrange("(o d) -> o d", o=1))

        transposes("a", 0)
        copies("a", 0)
        prep_until(3, XV_HEAD)
        quants("a", 0)
        prep_until(9, XV_HEAD)

        lim1 = chunk_parts(3)
        for k in range(NP + LAG + 3):
            jn, jh, ju = k - LAG, k - LAG - 1, k - LAG - 2
            todo = {"n": PACE[k]}

            def step():
                if todo["n"] > 0:
                    todo["n"] -= 1
                    prep(XV_1, lim1)

            if k + 1 < NP:
                load_x(k + 1)
            if k + 2 < NP:
                load_attn(k + 2)
            if k + 1 < NP:
                transposes("a", k + 1)
                copies("a", k + 1)
            if 0 <= jh < NP:
                transposes("h", jh)
            if k + 1 < NP:
                quants("a", k + 1)
            if 0 <= jh < NP:
                copies("h", jh)
                quants("h", jh)
            if k < NP:
                stage1_matmuls(k, lambda q: step() if (q in (1, 4) and ju < 0) else None)
            if k == 0:
                for g in range(G):
                    b = bank()
                    nc.tensor.matmul(b[:], lhsT=ones[:], rhs=grow[:, NW * g:NW * (g + 1)], start=True, stop=True)
                    nc.vector.tensor_copy(out=gsort[:, g].rearrange("p u (m e) -> p u m e", e=2),
                                          in_=b[:].rearrange("p (m u e) -> p u m e", u=2, e=2))
            units = []
            if 0 <= ju < NP:
                for t in (2 * ju, 2 * ju + 1):
                    units.append((0, t))
                    if k >= K1:
                        units.append((1, t))
            extras = []
            if k < NP:
                extras.append(lambda: squares(k, 1))
            if 0 <= jn < NP:
                extras.append(lambda: normed(jn, 0))
                extras.append(lambda: normed(jn, 1))
            if not units:
                for e in extras:
                    e()
            if units:
                prep_until(chunk_parts(2 if k >= K1 else 1), XV_1)
            for q, (c, t) in enumerate(units):
                unit(c, t)
                if q == 0:
                    for e in extras[0:2]:
                        e()
                elif q == 1:
                    for e in extras[2:]:
                        e()
                    step()
                else:
                    step()
        prep_until(chunk_parts(2), XV_1)
        for t in range(2 * (K1 - LAG - 2)):
            unit(1, t)
            if t % 2 == 0:
                prep(XV_2, chunk_parts(4))
        for c in range(2, NCH):
            prep_until(chunk_parts(c + 1), XV_2)
            for t in range(2 * NP):
                unit(c, t)
                if t % 3 == 2:
                    prep(XV_2, chunk_parts(c + 3))
